import numpy as np
import ml_dtypes

BF16 = ml_dtypes.bfloat16


def bf(x):
    return np.asarray(x, np.float32).astype(BF16)


def f32(x):
    return np.asarray(x, np.float32)


def f64(x):
    return np.asarray(x).astype(np.float64)


def striped(idx):
    return np.tile(idx.reshape(-1, 16).T, (8, 1))


S, D, Q, M, N = 4096, 128, 256, 512, 1024


def setup_inputs():
    return {"table": bf(np.random.standard_normal((D, S))), "w": bf(np.random.standard_normal((D, M)) / np.sqrt(D)), "offs": striped(np.random.permutation(np.tile(np.arange(S), 2))[:N])}


def reference(table, w, offs):
    idx = offs[:16].T.reshape(-1)
    p = f64(w).T @ f64(table)[:, idx]
    p[:Q] = p[:Q] * (1.0 / np.sqrt(D))
    return p

@@ -1,0 +1,48 @@
+import math
+
+import concourse.mybir as mybir
+
+P = 128
+S = 4096
+M = 512
+N = 1024
+PIECE = 512
+BLOCKS = M // P
+PIECES = N // PIECE
+QUERY_BLOCKS = 256 // P
+QUERY_FACTOR = 1.0 / math.sqrt(128.0)
+
+FLOPS = 2 * P * M * N
+
+BF16, F32, U16 = mybir.dt.bfloat16, mybir.dt.float32, mybir.dt.uint16
+COPY = mybir.ActivationFunctionType.Copy
+
+
+def tile_widthchartransformermlpheaderfastpos_kernel(tc, table, w, offs, out):
+    nc = tc.nc
+    with (
+        tc.tile_pool(name="held", bufs=1) as held,
+        tc.tile_pool(name="staging", bufs=BLOCKS * PIECES) as staging,
+        tc.psum_pool(name="psum", bufs=BLOCKS * PIECES) as psum,
+    ):
+        offsets = held.tile([P, N // 16], U16, name="offsets")
+        nc.sync.dma_start(offsets[:], offs)
+        weights = held.tile([P, M], BF16, name="weights")
+        nc.scalar.dma_start(weights[:], w)
+        window = held.tile([P, S], BF16, name="window")
+        nc.sync.dma_start(window[:], table)
+
+        for block in range(BLOCKS):
+            factor = QUERY_FACTOR if block < QUERY_BLOCKS else 1.0
+            rows = slice(block * P, (block + 1) * P)
+            for piece in range(PIECES):
+                columns = slice(piece * PIECE, (piece + 1) * PIECE)
+                picked = window[:].indirect(offsets[:, piece * (PIECE // 16) : (piece + 1) * (PIECE // 16)])
+                product = psum.tile([P, PIECE], F32, name="product")
+                nc.tensor.matmul(product[:], weights[:, rows], picked, start=True, stop=True)
+                scaled = staging.tile([P, PIECE], F32, name="scaled")
+                if piece % 2 == 0:
+                    nc.vector.tensor_scalar_mul(scaled[:], product[:], factor)
+                else:
+                    nc.scalar.activation(scaled[:], product[:], COPY, scale=factor)
+                nc.sync.dma_start(out[rows, columns], scaled[:])

@@ -11,6 +11,8 @@ BLOCKS = M // P
 PIECES = N // PIECE
 QUERY_BLOCKS = 256 // P
 QUERY_FACTOR = 1.0 / math.sqrt(128.0)
+PSUM_BANKS = 8
+WARM_UPS = 8
 
 FLOPS = 2 * P * M * N
 
@@ -23,7 +25,8 @@ def tile_widthchartransformermlpheaderfastpos_kernel(tc, table, w, offs, out):
     with (
         tc.tile_pool(name="held", bufs=1) as held,
         tc.tile_pool(name="staging", bufs=BLOCKS * PIECES) as staging,
-        tc.psum_pool(name="psum", bufs=BLOCKS * PIECES) as psum,
+        tc.psum_pool(name="spare", bufs=1) as spare,
+        tc.psum_pool(name="psum", bufs=PSUM_BANKS - 1) as psum,
     ):
         offsets = held.tile([P, N // 16], U16, name="offsets")
         nc.sync.dma_start(offsets[:], offs)
@@ -31,6 +34,12 @@ def tile_widthchartransformermlpheaderfastpos_kernel(tc, table, w, offs, out):
         nc.scalar.dma_start(weights[:], w)
         window = held.tile([P, S], BF16, name="window")
         nc.sync.dma_start(window[:], table)
+
+        zeros = held.tile([P, PIECE], BF16, name="zeros")
+        nc.vector.memset(zeros[:], 0.0)
+        unread = spare.tile([P, PIECE], F32, name="unread")
+        for turn in range(WARM_UPS):
+            nc.tensor.matmul(unread[:], zeros[:, 0:P], zeros[:], start=True, stop=True)
 
         for block in range(BLOCKS):
             factor = QUERY_FACTOR if block < QUERY_BLOCKS else 1.0

@@ -12,7 +12,8 @@ PIECES = N // PIECE
 QUERY_BLOCKS = 256 // P
 QUERY_FACTOR = 1.0 / math.sqrt(128.0)
 PSUM_BANKS = 8
-WARM_UPS = 8
+QUARTER = S // 4
+WARM_UPS = 4
 
 FLOPS = 2 * P * M * N
 
@@ -28,18 +29,23 @@ def tile_widthchartransformermlpheaderfastpos_kernel(tc, table, w, offs, out):
         tc.psum_pool(name="spare", bufs=1) as spare,
         tc.psum_pool(name="psum", bufs=PSUM_BANKS - 1) as psum,
     ):
+        window = held.tile([P, S], BF16, name="window")
+        for quarter in range(4):
+            columns = slice(quarter * QUARTER, (quarter + 1) * QUARTER)
+            nc.sync.dma_start(window[:, columns], table[:, columns])
         offsets = held.tile([P, N // 16], U16, name="offsets")
         nc.sync.dma_start(offsets[:], offs)
         weights = held.tile([P, M], BF16, name="weights")
         nc.scalar.dma_start(weights[:], w)
-        window = held.tile([P, S], BF16, name="window")
-        nc.sync.dma_start(window[:], table)
 
         zeros = held.tile([P, PIECE], BF16, name="zeros")
         nc.vector.memset(zeros[:], 0.0)
         unread = spare.tile([P, PIECE], F32, name="unread")
         for turn in range(WARM_UPS):
             nc.tensor.matmul(unread[:], zeros[:, 0:P], zeros[:], start=True, stop=True)
+        for quarter in range(3):
+            arrived = window[:, quarter * QUARTER : quarter * QUARTER + PIECE]
+            nc.tensor.matmul(unread[:], zeros[:, 0:P], arrived, start=True, stop=True)
 
         for block in range(BLOCKS):
             factor = QUERY_FACTOR if block < QUERY_BLOCKS else 1.0

@@ -7,6 +7,7 @@ S = 4096
 M = 512
 N = 1024
 PIECE = 512
+HALF = PIECE // 2
 BLOCKS = M // P
 PIECES = N // PIECE
 QUERY_BLOCKS = 256 // P
@@ -25,7 +26,7 @@ def tile_widthchartransformermlpheaderfastpos_kernel(tc, table, w, offs, out):
     nc = tc.nc
     with (
         tc.tile_pool(name="held", bufs=1) as held,
-        tc.tile_pool(name="staging", bufs=BLOCKS * PIECES) as staging,
+        tc.tile_pool(name="staging", bufs=2 * BLOCKS * PIECES) as staging,
         tc.psum_pool(name="spare", bufs=1) as spare,
         tc.psum_pool(name="psum", bufs=PSUM_BANKS - 1) as psum,
     ):
@@ -51,13 +52,14 @@ def tile_widthchartransformermlpheaderfastpos_kernel(tc, table, w, offs, out):
             factor = QUERY_FACTOR if block < QUERY_BLOCKS else 1.0
             rows = slice(block * P, (block + 1) * P)
             for piece in range(PIECES):
-                columns = slice(piece * PIECE, (piece + 1) * PIECE)
                 picked = window[:].indirect(offsets[:, piece * (PIECE // 16) : (piece + 1) * (PIECE // 16)])
                 product = psum.tile([P, PIECE], F32, name="product")
                 nc.tensor.matmul(product[:], weights[:, rows], picked, start=True, stop=True)
-                scaled = staging.tile([P, PIECE], F32, name="scaled")
-                if piece % 2 == 0:
-                    nc.vector.tensor_scalar_mul(scaled[:], product[:], factor)
-                else:
-                    nc.scalar.activation(scaled[:], product[:], COPY, scale=factor)
-                nc.sync.dma_start(out[rows, columns], scaled[:])
+                for half in range(2):
+                    scaled = staging.tile([P, HALF], F32, name="scaled")
+                    if piece % 2 == 0:
+                        nc.vector.tensor_scalar_mul(scaled[:], product[:, half * HALF : (half + 1) * HALF], factor)
+                    else:
+                        nc.scalar.activation(scaled[:], product[:, half * HALF : (half + 1) * HALF], COPY, scale=factor)
+                    first = piece * PIECE + half * HALF
+                    nc.sync.dma_start(out[rows, first : first + HALF], scaled[:])

@@ -12,9 +12,7 @@ BLOCKS = M // P
 PIECES = N // PIECE
 QUERY_BLOCKS = 256 // P
 QUERY_FACTOR = 1.0 / math.sqrt(128.0)
-PSUM_BANKS = 8
 QUARTER = S // 4
-WARM_UPS = 4
 
 FLOPS = 2 * P * M * N
 
@@ -27,8 +25,7 @@ def tile_widthchartransformermlpheaderfastpos_kernel(tc, table, w, offs, out):
     with (
         tc.tile_pool(name="held", bufs=1) as held,
         tc.tile_pool(name="staging", bufs=2 * BLOCKS * PIECES) as staging,
-        tc.psum_pool(name="spare", bufs=1) as spare,
-        tc.psum_pool(name="psum", bufs=PSUM_BANKS - 1) as psum,
+        tc.psum_pool(name="psum", bufs=BLOCKS * PIECES) as psum,
     ):
         window = held.tile([P, S], BF16, name="window")
         for quarter in range(4):
@@ -38,15 +35,6 @@ def tile_widthchartransformermlpheaderfastpos_kernel(tc, table, w, offs, out):
         nc.sync.dma_start(offsets[:], offs)
         weights = held.tile([P, M], BF16, name="weights")
         nc.scalar.dma_start(weights[:], w)
-
-        zeros = held.tile([P, PIECE], BF16, name="zeros")
-        nc.vector.memset(zeros[:], 0.0)
-        unread = spare.tile([P, PIECE], F32, name="unread")
-        for turn in range(WARM_UPS):
-            nc.tensor.matmul(unread[:], zeros[:, 0:P], zeros[:], start=True, stop=True)
-        for quarter in range(3):
-            arrived = window[:, quarter * QUARTER : quarter * QUARTER + PIECE]
-            nc.tensor.matmul(unread[:], zeros[:, 0:P], arrived, start=True, stop=True)
 
         for block in range(BLOCKS):
             factor = QUERY_FACTOR if block < QUERY_BLOCKS else 1.0

@@ -34,7 +34,8 @@ def tile_widthchartransformermlpheaderfastpos_kernel(tc, table, w, offs, out):
         offsets = held.tile([P, N // 16], U16, name="offsets")
         nc.sync.dma_start(offsets[:], offs)
         weights = held.tile([P, M], BF16, name="weights")
-        nc.scalar.dma_start(weights[:], w)
+        nc.scalar.dma_start(weights[:, 0:P], w[:, 0:P])
+        nc.sync.dma_start(weights[:, P:M], w[:, P:M])
 
         for block in range(BLOCKS):
             factor = QUERY_FACTOR if block < QUERY_BLOCKS else 1.0

@@ -12,7 +12,6 @@ BLOCKS = M // P
 PIECES = N // PIECE
 QUERY_BLOCKS = 256 // P
 QUERY_FACTOR = 1.0 / math.sqrt(128.0)
-QUARTER = S // 4
 
 FLOPS = 2 * P * M * N
 
@@ -28,9 +27,7 @@ def tile_widthchartransformermlpheaderfastpos_kernel(tc, table, w, offs, out):
         tc.psum_pool(name="psum", bufs=BLOCKS * PIECES) as psum,
     ):
         window = held.tile([P, S], BF16, name="window")
-        for quarter in range(4):
-            columns = slice(quarter * QUARTER, (quarter + 1) * QUARTER)
-            nc.sync.dma_start(window[:, columns], table[:, columns])
+        nc.sync.dma_start(window[:], table)
         offsets = held.tile([P, N // 16], U16, name="offsets")
         nc.sync.dma_start(offsets[:], offs)
         weights = held.tile([P, M], BF16, name="weights")

@@ -6,8 +6,9 @@ P = 128
 S = 4096
 M = 512
 N = 1024
-PIECE = 512
-HALF = PIECE // 2
+BANK = 512
+PSUM_BANKS = 8
+PIECE = 256
 BLOCKS = M // P
 PIECES = N // PIECE
 QUERY_BLOCKS = 256 // P
@@ -23,8 +24,8 @@ def tile_widthchartransformermlpheaderfastpos_kernel(tc, table, w, offs, out):
     nc = tc.nc
     with (
         tc.tile_pool(name="held", bufs=1) as held,
-        tc.tile_pool(name="staging", bufs=2 * BLOCKS * PIECES) as staging,
-        tc.psum_pool(name="psum", bufs=BLOCKS * PIECES) as psum,
+        tc.tile_pool(name="staging", bufs=BLOCKS * PIECES) as staging,
+        tc.psum_pool(name="psum", bufs=PSUM_BANKS) as psum,
     ):
         window = held.tile([P, S], BF16, name="window")
         nc.sync.dma_start(window[:], table)
@@ -39,13 +40,11 @@ def tile_widthchartransformermlpheaderfastpos_kernel(tc, table, w, offs, out):
             rows = slice(block * P, (block + 1) * P)
             for piece in range(PIECES):
                 picked = window[:].indirect(offsets[:, piece * (PIECE // 16) : (piece + 1) * (PIECE // 16)])
-                product = psum.tile([P, PIECE], F32, name="product")
-                nc.tensor.matmul(product[:], weights[:, rows], picked, start=True, stop=True)
-                for half in range(2):
-                    scaled = staging.tile([P, HALF], F32, name="scaled")
-                    if piece % 2 == 0:
-                        nc.vector.tensor_scalar_mul(scaled[:], product[:, half * HALF : (half + 1) * HALF], factor)
-                    else:
-                        nc.scalar.activation(scaled[:], product[:, half * HALF : (half + 1) * HALF], COPY, scale=factor)
-                    first = piece * PIECE + half * HALF
-                    nc.sync.dma_start(out[rows, first : first + HALF], scaled[:])
+                product = psum.tile([P, BANK], F32, name="product")
+                nc.tensor.matmul(product[:, 0:PIECE], weights[:, rows], picked, start=True, stop=True)
+                scaled = staging.tile([P, PIECE], F32, name="scaled")
+                if piece % 2 == 0:
+                    nc.vector.tensor_scalar_mul(scaled[:], product[:, 0:PIECE], factor)
+                else:
+                    nc.scalar.activation(scaled[:], product[:, 0:PIECE], COPY, scale=factor)
+                nc.sync.dma_start(out[rows, piece * PIECE : (piece + 1) * PIECE], scaled[:])

@@ -17,7 +17,6 @@ QUERY_FACTOR = 1.0 / math.sqrt(128.0)
 FLOPS = 2 * P * M * N
 
 BF16, F32, U16 = mybir.dt.bfloat16, mybir.dt.float32, mybir.dt.uint16
-COPY = mybir.ActivationFunctionType.Copy
 
 
 def tile_widthchartransformermlpheaderfastpos_kernel(tc, table, w, offs, out):
@@ -43,8 +42,5 @@ def tile_widthchartransformermlpheaderfastpos_kernel(tc, table, w, offs, out):
                 product = psum.tile([P, BANK], F32, name="product")
                 nc.tensor.matmul(product[:, 0:PIECE], weights[:, rows], picked, start=True, stop=True)
                 scaled = staging.tile([P, PIECE], F32, name="scaled")
-                if piece % 2 == 0:
-                    nc.vector.tensor_scalar_mul(scaled[:], product[:, 0:PIECE], factor)
-                else:
-                    nc.scalar.activation(scaled[:], product[:, 0:PIECE], COPY, scale=factor)
+                nc.vector.tensor_scalar_mul(scaled[:], product[:, 0:PIECE], factor)
                 nc.sync.dma_start(out[rows, piece * PIECE : (piece + 1) * PIECE], scaled[:])

import math

import concourse.mybir as mybir

P = 128
S = 4096
M = 512
N = 1024
BANK = 512
PSUM_BANKS = 8
PIECE = 256
BLOCKS = M // P
PIECES = N // PIECE
QUERY_BLOCKS = 256 // P
QUERY_FACTOR = 1.0 / math.sqrt(128.0)

FLOPS = 2 * P * M * N

BF16, F32, U16 = mybir.dt.bfloat16, mybir.dt.float32, mybir.dt.uint16


def tile_widthchartransformermlpheaderfastpos_kernel(tc, table, w, offs, out):
    nc = tc.nc
    with (
        tc.tile_pool(name="held", bufs=1) as held,
        tc.tile_pool(name="staging", bufs=BLOCKS * PIECES) as staging,
        tc.psum_pool(name="psum", bufs=PSUM_BANKS) as psum,
    ):
        window = held.tile([P, S], BF16, name="window")
        nc.sync.dma_start(window[:], table)
        offsets = held.tile([P, N // 16], U16, name="offsets")
        nc.sync.dma_start(offsets[:], offs)
        weights = held.tile([P, M], BF16, name="weights")
        nc.scalar.dma_start(weights[:, 0:P], w[:, 0:P])
        nc.sync.dma_start(weights[:, P:M], w[:, P:M])

        for block in range(BLOCKS):
            factor = QUERY_FACTOR if block < QUERY_BLOCKS else 1.0
            rows = slice(block * P, (block + 1) * P)
            for piece in range(PIECES):
                picked = window[:].indirect(offsets[:, piece * (PIECE // 16) : (piece + 1) * (PIECE // 16)])
                product = psum.tile([P, BANK], F32, name="product")
                nc.tensor.matmul(product[:, 0:PIECE], weights[:, rows], picked, start=True, stop=True)
                scaled = staging.tile([P, PIECE], F32, name="scaled")
                nc.vector.tensor_scalar_mul(scaled[:], product[:, 0:PIECE], factor)
                nc.sync.dma_start(out[rows, piece * PIECE : (piece + 1) * PIECE], scaled[:])
